import numpy as np
import ml_dtypes

BF16 = ml_dtypes.bfloat16


def bf(x):
    return np.asarray(x, np.float32).astype(BF16)


def f32(x):
    return np.asarray(x, np.float32)


def f64(x):
    return np.asarray(x).astype(np.float64)


def striped(idx):
    return np.tile(idx.reshape(-1, 16).T, (8, 1))


D, S, K, M, N = 128, 2048, 4, 128, 8192


def xavier(rows, cols):
    lim = np.sqrt(6.0 / (2 * D + M))
    return np.random.uniform(-lim, lim, (rows, cols))


def setup_inputs():
    return {"x": bf(np.random.standard_normal((D, S))), "w_self": bf(xavier(D, M)), "w_nb": bf(xavier(D, M)), "offs": striped(np.concatenate([np.random.permutation(S) for _ in range(K)]))}


def reference(x, w_self, w_nb, offs):
    idx = offs[:16].T.reshape(-1)
    xx = f64(x)
    agg = xx[:, idx].reshape(D, K, S).mean(axis=1)
    return np.maximum(f64(w_self).T @ xx + f64(w_nb).T @ agg, 0.0)

@@ -1,0 +1,63 @@
+import concourse.mybir as mybir
+
+BF16 = mybir.dt.bfloat16
+F32 = mybir.dt.float32
+U16 = mybir.dt.uint16
+MULT = mybir.AluOpType.mult
+MAX = mybir.AluOpType.max
+
+P = 128
+NODES = 2048
+NEIGHBOURS = 4
+BLOCK = 512
+PER_COLUMN = 16
+
+FLOPS = 2 * P * P * NODES * (1 + NEIGHBOURS)
+
+
+def tile_graphsage_kernel(tc, x, w_self, w_nb, offs, out):
+    nc = tc.nc
+    with (
+        tc.tile_pool(name="held", bufs=1) as held,
+        tc.tile_pool(name="results", bufs=2) as results,
+        tc.psum_pool(name="banks", bufs=1) as banks,
+    ):
+        offsets = held.tile([P, NEIGHBOURS * NODES // PER_COLUMN], U16, name="offsets")
+        nc.sync.dma_start(offsets[:], offs)
+        features = held.tile([P, NODES], BF16, name="features")
+        nc.scalar.dma_start(features[:], x)
+        own_weights = held.tile([P, P], BF16, name="own_weights")
+        nc.sync.dma_start(own_weights[:], w_self)
+        neighbour_weights = held.tile([P, P], BF16, name="neighbour_weights")
+        nc.sync.dma_start(neighbour_weights[:], w_nb)
+
+        own_weights_x4 = held.tile([P, P], BF16, name="own_weights_x4")
+        nc.vector.tensor_scalar_mul(own_weights_x4[:], own_weights[:], float(NEIGHBOURS))
+
+        blocks = range(NODES // BLOCK)
+        bank = [banks.tile([P, BLOCK], F32, name=f"bank{b}") for b in blocks]
+        for b in blocks:
+            nc.tensor.matmul(
+                bank[b][:],
+                own_weights_x4[:],
+                features[:, b * BLOCK : (b + 1) * BLOCK],
+                start=True,
+                stop=False,
+            )
+
+        for b in blocks:
+            for k in range(NEIGHBOURS):
+                first_column = (k * NODES + b * BLOCK) // PER_COLUMN
+                picked = features[:].indirect(
+                    offsets[:, first_column : first_column + BLOCK // PER_COLUMN]
+                )
+                nc.tensor.matmul(
+                    bank[b][:],
+                    neighbour_weights[:],
+                    picked,
+                    start=False,
+                    stop=(k == NEIGHBOURS - 1),
+                )
+            result = results.tile([P, BLOCK], F32, name="result")
+            nc.vector.tensor_scalar(result[:], bank[b][:], 1.0 / NEIGHBOURS, 0.0, MULT, MAX)
+            nc.sync.dma_start(out[:, b * BLOCK : (b + 1) * BLOCK], result[:])

@@ -22,19 +22,24 @@ def tile_graphsage_kernel(tc, x, w_self, w_nb, offs, out):
         tc.tile_pool(name="results", bufs=2) as results,
         tc.psum_pool(name="banks", bufs=1) as banks,
     ):
+        blocks = range(NODES // BLOCK)
+
+        own_weights = held.tile([P, P], BF16, name="own_weights")
+        nc.scalar.dma_start(own_weights[:], w_self)
         offsets = held.tile([P, NEIGHBOURS * NODES // PER_COLUMN], U16, name="offsets")
         nc.sync.dma_start(offsets[:], offs)
         features = held.tile([P, NODES], BF16, name="features")
-        nc.scalar.dma_start(features[:], x)
-        own_weights = held.tile([P, P], BF16, name="own_weights")
-        nc.sync.dma_start(own_weights[:], w_self)
+        for b in blocks:
+            queue = nc.scalar if b < len(blocks) // 2 else nc.sync
+            queue.dma_start(
+                features[:, b * BLOCK : (b + 1) * BLOCK], x[:, b * BLOCK : (b + 1) * BLOCK]
+            )
         neighbour_weights = held.tile([P, P], BF16, name="neighbour_weights")
-        nc.sync.dma_start(neighbour_weights[:], w_nb)
+        nc.scalar.dma_start(neighbour_weights[:], w_nb)
 
         own_weights_x4 = held.tile([P, P], BF16, name="own_weights_x4")
         nc.vector.tensor_scalar_mul(own_weights_x4[:], own_weights[:], float(NEIGHBOURS))
 
-        blocks = range(NODES // BLOCK)
         bank = [banks.tile([P, BLOCK], F32, name=f"bank{b}") for b in blocks]
         for b in blocks:
             nc.tensor.matmul(

@@ -10,6 +10,7 @@ P = 128
 NODES = 2048
 NEIGHBOURS = 4
 BLOCK = 512
+WARM_UP_MATMULS = 5
 PER_COLUMN = 16
 
 FLOPS = 2 * P * P * NODES * (1 + NEIGHBOURS)
@@ -36,6 +37,12 @@ def tile_graphsage_kernel(tc, x, w_self, w_nb, offs, out):
             )
         neighbour_weights = held.tile([P, P], BF16, name="neighbour_weights")
         nc.scalar.dma_start(neighbour_weights[:], w_nb)
+
+        zeros = held.tile([P, BLOCK], BF16, name="zeros")
+        nc.vector.memset(zeros[:], 0.0)
+        unread_bank = banks.tile([P, BLOCK], F32, name="unread_bank")
+        for i in range(WARM_UP_MATMULS):
+            nc.tensor.matmul(unread_bank[:], zeros[:, 0:P], zeros[:], start=True, stop=True)
 
         own_weights_x4 = held.tile([P, P], BF16, name="own_weights_x4")
         nc.vector.tensor_scalar_mul(own_weights_x4[:], own_weights[:], float(NEIGHBOURS))

@@ -10,6 +10,7 @@ P = 128
 NODES = 2048
 NEIGHBOURS = 4
 BLOCK = 512
+HALF = BLOCK // 2
 WARM_UP_MATMULS = 5
 PER_COLUMN = 16
 
@@ -20,7 +21,7 @@ def tile_graphsage_kernel(tc, x, w_self, w_nb, offs, out):
     nc = tc.nc
     with (
         tc.tile_pool(name="held", bufs=1) as held,
-        tc.tile_pool(name="results", bufs=2) as results,
+        tc.tile_pool(name="results", bufs=4) as results,
         tc.psum_pool(name="banks", bufs=1) as banks,
     ):
         blocks = range(NODES // BLOCK)
@@ -70,6 +71,15 @@ def tile_graphsage_kernel(tc, x, w_self, w_nb, offs, out):
                     start=False,
                     stop=(k == NEIGHBOURS - 1),
                 )
-            result = results.tile([P, BLOCK], F32, name="result")
-            nc.vector.tensor_scalar(result[:], bank[b][:], 1.0 / NEIGHBOURS, 0.0, MULT, MAX)
-            nc.sync.dma_start(out[:, b * BLOCK : (b + 1) * BLOCK], result[:])
+            for half, queue in enumerate((nc.sync, nc.scalar)):
+                result = results.tile([P, HALF], F32, name="result")
+                nc.vector.tensor_scalar(
+                    result[:],
+                    bank[b][:, half * HALF : (half + 1) * HALF],
+                    1.0 / NEIGHBOURS,
+                    0.0,
+                    MULT,
+                    MAX,
+                )
+                first_node = b * BLOCK + half * HALF
+                queue.dma_start(out[:, first_node : first_node + HALF], result[:])

@@ -10,8 +10,7 @@ P = 128
 NODES = 2048
 NEIGHBOURS = 4
 BLOCK = 512
-HALF = BLOCK // 2
-WARM_UP_MATMULS = 5
+WARM_UP_MATMULS = 20
 PER_COLUMN = 16
 
 FLOPS = 2 * P * P * NODES * (1 + NEIGHBOURS)
@@ -21,7 +20,7 @@ def tile_graphsage_kernel(tc, x, w_self, w_nb, offs, out):
     nc = tc.nc
     with (
         tc.tile_pool(name="held", bufs=1) as held,
-        tc.tile_pool(name="results", bufs=4) as results,
+        tc.tile_pool(name="results", bufs=2) as results,
         tc.psum_pool(name="banks", bufs=1) as banks,
     ):
         blocks = range(NODES // BLOCK)
@@ -39,11 +38,11 @@ def tile_graphsage_kernel(tc, x, w_self, w_nb, offs, out):
         neighbour_weights = held.tile([P, P], BF16, name="neighbour_weights")
         nc.scalar.dma_start(neighbour_weights[:], w_nb)
 
-        zeros = held.tile([P, BLOCK], BF16, name="zeros")
+        zeros = held.tile([P, P], BF16, name="zeros")
         nc.vector.memset(zeros[:], 0.0)
-        unread_bank = banks.tile([P, BLOCK], F32, name="unread_bank")
+        unread_bank = banks.tile([P, P], F32, name="unread_bank")
         for i in range(WARM_UP_MATMULS):
-            nc.tensor.matmul(unread_bank[:], zeros[:, 0:P], zeros[:], start=True, stop=True)
+            nc.tensor.matmul(unread_bank[:], zeros[:], zeros[:], start=True, stop=True)
 
         own_weights_x4 = held.tile([P, P], BF16, name="own_weights_x4")
         nc.vector.tensor_scalar_mul(own_weights_x4[:], own_weights[:], float(NEIGHBOURS))
@@ -71,15 +70,6 @@ def tile_graphsage_kernel(tc, x, w_self, w_nb, offs, out):
                     start=False,
                     stop=(k == NEIGHBOURS - 1),
                 )
-            for half, queue in enumerate((nc.sync, nc.scalar)):
-                result = results.tile([P, HALF], F32, name="result")
-                nc.vector.tensor_scalar(
-                    result[:],
-                    bank[b][:, half * HALF : (half + 1) * HALF],
-                    1.0 / NEIGHBOURS,
-                    0.0,
-                    MULT,
-                    MAX,
-                )
-                first_node = b * BLOCK + half * HALF
-                queue.dma_start(out[:, first_node : first_node + HALF], result[:])
+            result = results.tile([P, BLOCK], F32, name="result")
+            nc.vector.tensor_scalar(result[:], bank[b][:], 1.0 / NEIGHBOURS, 0.0, MULT, MAX)
+            nc.sync.dma_start(out[:, b * BLOCK : (b + 1) * BLOCK], result[:])

@@ -3,14 +3,13 @@ import concourse.mybir as mybir
 BF16 = mybir.dt.bfloat16
 F32 = mybir.dt.float32
 U16 = mybir.dt.uint16
-MULT = mybir.AluOpType.mult
-MAX = mybir.AluOpType.max
+RELU = mybir.ActivationFunctionType.Relu
 
 P = 128
 NODES = 2048
 NEIGHBOURS = 4
 BLOCK = 512
-WARM_UP_MATMULS = 20
+WARM_UP_MATMULS = 5
 PER_COLUMN = 16
 
 FLOPS = 2 * P * P * NODES * (1 + NEIGHBOURS)
@@ -38,11 +37,11 @@ def tile_graphsage_kernel(tc, x, w_self, w_nb, offs, out):
         neighbour_weights = held.tile([P, P], BF16, name="neighbour_weights")
         nc.scalar.dma_start(neighbour_weights[:], w_nb)
 
-        zeros = held.tile([P, P], BF16, name="zeros")
+        zeros = held.tile([P, BLOCK], BF16, name="zeros")
         nc.vector.memset(zeros[:], 0.0)
-        unread_bank = banks.tile([P, P], F32, name="unread_bank")
+        unread_bank = banks.tile([P, BLOCK], F32, name="unread_bank")
         for i in range(WARM_UP_MATMULS):
-            nc.tensor.matmul(unread_bank[:], zeros[:], zeros[:], start=True, stop=True)
+            nc.tensor.matmul(unread_bank[:], zeros[:, 0:P], zeros[:], start=True, stop=True)
 
         own_weights_x4 = held.tile([P, P], BF16, name="own_weights_x4")
         nc.vector.tensor_scalar_mul(own_weights_x4[:], own_weights[:], float(NEIGHBOURS))
@@ -71,5 +70,5 @@ def tile_graphsage_kernel(tc, x, w_self, w_nb, offs, out):
                     stop=(k == NEIGHBOURS - 1),
                 )
             result = results.tile([P, BLOCK], F32, name="result")
-            nc.vector.tensor_scalar(result[:], bank[b][:], 1.0 / NEIGHBOURS, 0.0, MULT, MAX)
-            nc.sync.dma_start(out[:, b * BLOCK : (b + 1) * BLOCK], result[:])
+            nc.scalar.activation(result[:], bank[b][:], RELU, scale=1.0 / NEIGHBOURS)
+            nc.scalar.dma_start(out[:, b * BLOCK : (b + 1) * BLOCK], result[:])

@@ -9,7 +9,7 @@ P = 128
 NODES = 2048
 NEIGHBOURS = 4
 BLOCK = 512
-WARM_UP_MATMULS = 5
+WARM_UP_MATMULS = 3
 PER_COLUMN = 16
 
 FLOPS = 2 * P * P * NODES * (1 + NEIGHBOURS)
@@ -26,14 +26,14 @@ def tile_graphsage_kernel(tc, x, w_self, w_nb, offs, out):
 
         own_weights = held.tile([P, P], BF16, name="own_weights")
         nc.scalar.dma_start(own_weights[:], w_self)
-        offsets = held.tile([P, NEIGHBOURS * NODES // PER_COLUMN], U16, name="offsets")
-        nc.sync.dma_start(offsets[:], offs)
         features = held.tile([P, NODES], BF16, name="features")
         for b in blocks:
             queue = nc.scalar if b < len(blocks) // 2 else nc.sync
             queue.dma_start(
                 features[:, b * BLOCK : (b + 1) * BLOCK], x[:, b * BLOCK : (b + 1) * BLOCK]
             )
+        offsets = held.tile([P, NEIGHBOURS * NODES // PER_COLUMN], U16, name="offsets")
+        nc.sync.dma_start(offsets[:], offs)
         neighbour_weights = held.tile([P, P], BF16, name="neighbour_weights")
         nc.scalar.dma_start(neighbour_weights[:], w_nb)
 

@@ -9,7 +9,7 @@ P = 128
 NODES = 2048
 NEIGHBOURS = 4
 BLOCK = 512
-WARM_UP_MATMULS = 3
+WARM_UP_MATMULS = 4
 PER_COLUMN = 16
 
 FLOPS = 2 * P * P * NODES * (1 + NEIGHBOURS)
@@ -37,11 +37,17 @@ def tile_graphsage_kernel(tc, x, w_self, w_nb, offs, out):
         neighbour_weights = held.tile([P, P], BF16, name="neighbour_weights")
         nc.scalar.dma_start(neighbour_weights[:], w_nb)
 
-        zeros = held.tile([P, BLOCK], BF16, name="zeros")
+        zeros = held.tile([P, P], BF16, name="zeros")
         nc.vector.memset(zeros[:], 0.0)
         unread_bank = banks.tile([P, BLOCK], F32, name="unread_bank")
         for i in range(WARM_UP_MATMULS):
-            nc.tensor.matmul(unread_bank[:], zeros[:, 0:P], zeros[:], start=True, stop=True)
+            nc.tensor.matmul(
+                unread_bank[:],
+                zeros[:],
+                zeros[:].unsqueeze(1).to_broadcast([P, BLOCK // P, P]),
+                start=True,
+                stop=True,
+            )
 
         own_weights_x4 = held.tile([P, P], BF16, name="own_weights_x4")
         nc.vector.tensor_scalar_mul(own_weights_x4[:], own_weights[:], float(NEIGHBOURS))

@@ -9,6 +9,7 @@ P = 128
 NODES = 2048
 NEIGHBOURS = 4
 BLOCK = 512
+HALF = BLOCK // 2
 WARM_UP_MATMULS = 4
 PER_COLUMN = 16
 
@@ -19,7 +20,7 @@ def tile_graphsage_kernel(tc, x, w_self, w_nb, offs, out):
     nc = tc.nc
     with (
         tc.tile_pool(name="held", bufs=1) as held,
-        tc.tile_pool(name="results", bufs=2) as results,
+        tc.tile_pool(name="results", bufs=4) as results,
         tc.psum_pool(name="banks", bufs=1) as banks,
     ):
         blocks = range(NODES // BLOCK)
@@ -75,6 +76,10 @@ def tile_graphsage_kernel(tc, x, w_self, w_nb, offs, out):
                     start=False,
                     stop=(k == NEIGHBOURS - 1),
                 )
-            result = results.tile([P, BLOCK], F32, name="result")
-            nc.scalar.activation(result[:], bank[b][:], RELU, scale=1.0 / NEIGHBOURS)
-            nc.scalar.dma_start(out[:, b * BLOCK : (b + 1) * BLOCK], result[:])
+            for h in range(2):
+                result = results.tile([P, HALF], F32, name="result")
+                nc.scalar.activation(
+                    result[:], bank[b][:, h * HALF : (h + 1) * HALF], RELU, scale=1.0 / NEIGHBOURS
+                )
+                first_node = b * BLOCK + h * HALF
+                nc.scalar.dma_start(out[:, first_node : first_node + HALF], result[:])

@@ -29,7 +29,7 @@ def tile_graphsage_kernel(tc, x, w_self, w_nb, offs, out):
         nc.scalar.dma_start(own_weights[:], w_self)
         features = held.tile([P, NODES], BF16, name="features")
         for b in blocks:
-            queue = nc.scalar if b < len(blocks) // 2 else nc.sync
+            queue = nc.sync if b % 2 == 0 else nc.scalar
             queue.dma_start(
                 features[:, b * BLOCK : (b + 1) * BLOCK], x[:, b * BLOCK : (b + 1) * BLOCK]
             )

@@ -20,7 +20,7 @@ def tile_graphsage_kernel(tc, x, w_self, w_nb, offs, out):
     nc = tc.nc
     with (
         tc.tile_pool(name="held", bufs=1) as held,
-        tc.tile_pool(name="results", bufs=4) as results,
+        tc.tile_pool(name="results", bufs=8) as results,
         tc.psum_pool(name="banks", bufs=1) as banks,
     ):
         blocks = range(NODES // BLOCK)

@@ -3,7 +3,7 @@ import concourse.mybir as mybir
 BF16 = mybir.dt.bfloat16
 F32 = mybir.dt.float32
 U16 = mybir.dt.uint16
-RELU = mybir.ActivationFunctionType.Relu
+MULT, MAX = mybir.AluOpType.mult, mybir.AluOpType.max
 
 P = 128
 NODES = 2048
@@ -78,8 +78,8 @@ def tile_graphsage_kernel(tc, x, w_self, w_nb, offs, out):
                 )
             for h in range(2):
                 result = results.tile([P, HALF], F32, name="result")
-                nc.scalar.activation(
-                    result[:], bank[b][:, h * HALF : (h + 1) * HALF], RELU, scale=1.0 / NEIGHBOURS
+                nc.vector.tensor_scalar(
+                    result[:], bank[b][:, h * HALF : (h + 1) * HALF], 1.0 / NEIGHBOURS, 0.0, MULT, MAX
                 )
                 first_node = b * BLOCK + h * HALF
-                nc.scalar.dma_start(out[:, first_node : first_node + HALF], result[:])
+                nc.sync.dma_start(out[:, first_node : first_node + HALF], result[:])

@@ -82,4 +82,4 @@ def tile_graphsage_kernel(tc, x, w_self, w_nb, offs, out):
                     result[:], bank[b][:, h * HALF : (h + 1) * HALF], 1.0 / NEIGHBOURS, 0.0, MULT, MAX
                 )
                 first_node = b * BLOCK + h * HALF
-                nc.sync.dma_start(out[:, first_node : first_node + HALF], result[:])
+                nc.scalar.dma_start(out[:, first_node : first_node + HALF], result[:])

@@ -10,6 +10,7 @@ NODES = 2048
 NEIGHBOURS = 4
 BLOCK = 512
 HALF = BLOCK // 2
+THIRD = 176
 WARM_UP_MATMULS = 4
 PER_COLUMN = 16
 
@@ -20,7 +21,7 @@ def tile_graphsage_kernel(tc, x, w_self, w_nb, offs, out):
     nc = tc.nc
     with (
         tc.tile_pool(name="held", bufs=1) as held,
-        tc.tile_pool(name="results", bufs=8) as results,
+        tc.tile_pool(name="results", bufs=1) as results,
         tc.psum_pool(name="banks", bufs=1) as banks,
     ):
         blocks = range(NODES // BLOCK)
@@ -76,10 +77,11 @@ def tile_graphsage_kernel(tc, x, w_self, w_nb, offs, out):
                     start=False,
                     stop=(k == NEIGHBOURS - 1),
                 )
-            for h in range(2):
-                result = results.tile([P, HALF], F32, name="result")
+            step = THIRD if b == blocks[-1] else HALF
+            for first in range(0, BLOCK, step):
+                last = min(first + step, BLOCK)
+                result = results.tile([P, last - first], F32, name=f"result{b}_{first}")
                 nc.vector.tensor_scalar(
-                    result[:], bank[b][:, h * HALF : (h + 1) * HALF], 1.0 / NEIGHBOURS, 0.0, MULT, MAX
+                    result[:], bank[b][:, first:last], 1.0 / NEIGHBOURS, 0.0, MULT, MAX
                 )
-                first_node = b * BLOCK + h * HALF
-                nc.scalar.dma_start(out[:, first_node : first_node + HALF], result[:])
+                nc.scalar.dma_start(out[:, b * BLOCK + first : b * BLOCK + last], result[:])

import concourse.mybir as mybir

BF16 = mybir.dt.bfloat16
F32 = mybir.dt.float32
U16 = mybir.dt.uint16
MULT, MAX = mybir.AluOpType.mult, mybir.AluOpType.max

P = 128
NODES = 2048
NEIGHBOURS = 4
BLOCK = 512
HALF = BLOCK // 2
THIRD = 176
WARM_UP_MATMULS = 4
PER_COLUMN = 16

FLOPS = 2 * P * P * NODES * (1 + NEIGHBOURS)


def tile_graphsage_kernel(tc, x, w_self, w_nb, offs, out):
    nc = tc.nc
    with (
        tc.tile_pool(name="held", bufs=1) as held,
        tc.tile_pool(name="results", bufs=1) as results,
        tc.psum_pool(name="banks", bufs=1) as banks,
    ):
        blocks = range(NODES // BLOCK)

        own_weights = held.tile([P, P], BF16, name="own_weights")
        nc.scalar.dma_start(own_weights[:], w_self)
        features = held.tile([P, NODES], BF16, name="features")
        for b in blocks:
            queue = nc.sync if b % 2 == 0 else nc.scalar
            queue.dma_start(
                features[:, b * BLOCK : (b + 1) * BLOCK], x[:, b * BLOCK : (b + 1) * BLOCK]
            )
        offsets = held.tile([P, NEIGHBOURS * NODES // PER_COLUMN], U16, name="offsets")
        nc.sync.dma_start(offsets[:], offs)
        neighbour_weights = held.tile([P, P], BF16, name="neighbour_weights")
        nc.scalar.dma_start(neighbour_weights[:], w_nb)

        zeros = held.tile([P, P], BF16, name="zeros")
        nc.vector.memset(zeros[:], 0.0)
        unread_bank = banks.tile([P, BLOCK], F32, name="unread_bank")
        for i in range(WARM_UP_MATMULS):
            nc.tensor.matmul(
                unread_bank[:],
                zeros[:],
                zeros[:].unsqueeze(1).to_broadcast([P, BLOCK // P, P]),
                start=True,
                stop=True,
            )

        own_weights_x4 = held.tile([P, P], BF16, name="own_weights_x4")
        nc.vector.tensor_scalar_mul(own_weights_x4[:], own_weights[:], float(NEIGHBOURS))

        bank = [banks.tile([P, BLOCK], F32, name=f"bank{b}") for b in blocks]
        for b in blocks:
            nc.tensor.matmul(
                bank[b][:],
                own_weights_x4[:],
                features[:, b * BLOCK : (b + 1) * BLOCK],
                start=True,
                stop=False,
            )

        for b in blocks:
            for k in range(NEIGHBOURS):
                first_column = (k * NODES + b * BLOCK) // PER_COLUMN
                picked = features[:].indirect(
                    offsets[:, first_column : first_column + BLOCK // PER_COLUMN]
                )
                nc.tensor.matmul(
                    bank[b][:],
                    neighbour_weights[:],
                    picked,
                    start=False,
                    stop=(k == NEIGHBOURS - 1),
                )
            step = THIRD if b == blocks[-1] else HALF
            for first in range(0, BLOCK, step):
                last = min(first + step, BLOCK)
                result = results.tile([P, last - first], F32, name=f"result{b}_{first}")
                nc.vector.tensor_scalar(
                    result[:], bank[b][:, first:last], 1.0 / NEIGHBOURS, 0.0, MULT, MAX
                )
                nc.scalar.dma_start(out[:, b * BLOCK + first : b * BLOCK + last], result[:])
